import numpy as np
import ml_dtypes


def mxq(x, axis, fmt="e4m3"):
    dtype, down = {"e4m3": (ml_dtypes.float8_e4m3fn, 7), "e5m2": (ml_dtypes.float8_e5m2, 14)}[fmt]
    v = np.moveaxis(np.asarray(x, np.float32).astype(ml_dtypes.bfloat16).astype(np.float64), axis, -1)
    blocks = v.reshape(v.shape[:-1] + (-1, 32))
    amax = np.abs(blocks).max(-1, keepdims=True)
    byte = np.maximum(np.where(amax > 0, np.frexp(amax)[1] - 1 + 127, 0) - down, 1)
    scale = np.exp2(byte - 127.0)
    codes = (blocks / scale).astype(np.float32).astype(dtype).astype(np.float64)
    return np.moveaxis((codes * scale).reshape(v.shape), -1, axis)


WIDE = False


def mx_kscale(k):
    if not WIDE:
        return np.ones(k)
    levels = np.array([10, -10, 5, -5, 0])
    if k % 512:
        return np.exp2(np.random.permutation(np.resize(levels, k // 32))).repeat(32)
    a = np.empty((k // 512, 16))
    for p in range(k // 512):
        a[p, :8] = np.random.permutation(np.resize(levels, 8))
        for g in range(8):
            far = levels[np.abs(levels - a[p, g]) >= 10]
            a[p, g + 8] = far[np.random.randint(len(far))]
    return np.exp2(a.ravel()).repeat(32)


BF16 = ml_dtypes.bfloat16


def bf(x):
    return np.asarray(x, np.float32).astype(BF16)


def f64(x):
    return np.asarray(x).astype(np.float64)


B, T, C_IN, HIDDEN, HEADS, OUT_DIM = 4, 2048, 512, 512, 8, 512
RMS_EPS = 1.1920928955078125e-07


def silu(z):
    return z / (1.0 + np.exp(-z))


def draw0():
    s, t = mx_kscale(C_IN), mx_kscale(HIDDEN)
    r = np.exp2(-12.0 * np.random.random((B, T, 1)))
    return {"x": bf(np.random.standard_normal((B, T, C_IN)) * s),
            "h_attn": bf(np.random.standard_normal((B, T, HIDDEN)) * 0.8 * r),
            "Wu": bf(np.random.standard_normal((HIDDEN, C_IN)) / np.sqrt(C_IN) / s),
            "bu": bf(np.random.standard_normal(HIDDEN) * 0.1),
            "g_norm": bf((1.0 + 0.1 * np.random.standard_normal(HIDDEN)) * t),
            "Wf": bf(np.random.standard_normal((OUT_DIM, HIDDEN)) / np.sqrt(HIDDEN) / t),
            "b_out": bf(np.random.standard_normal(OUT_DIM) * 0.1)}


def core(x, h_attn, Wu, bu, g_norm, Wf, b_out):
    u = silu((mxq(f64(x), 2, "e4m3") @ mxq(f64(Wu), 1, "e4m3").T) + f64(bu))
    av = f64(h_attn)
    av_norm = av * (1.0 / np.sqrt(np.mean(av * av, axis=-1, keepdims=True) + RMS_EPS)) * f64(g_norm)
    uv = av_norm * u
    return (mxq(uv, 2, "e4m3") @ mxq(f64(Wf), 1, "e4m3").T) + f64(b_out)


def e4m3fn_bytes(y):
    return np.clip(np.asarray(y, np.float64), -448.0, 448.0).astype(np.float32).astype(ml_dtypes.float8_e4m3fn).view(np.uint8)


def e4m3fn_values(b):
    return np.asarray(b, np.uint8).view(ml_dtypes.float8_e4m3fn).astype(np.float64)


def setup_inputs():
    d = draw0()
    x0 = np.asarray(d['x']).astype(np.float64)
    s = (np.max(np.abs(x0), axis=(0, 1), keepdims=True) / 448.0).astype(np.float32)
    out = {}
    for k, v in d.items():
        if k == 'x':
            out['x_bytes'] = e4m3fn_bytes(x0 / s.astype(np.float64))
            out['x_scale'] = s
        else:
            out[k] = v
    return out


def reference(x_bytes, x_scale, h_attn, Wu, bu, g_norm, Wf, b_out):
    return core(e4m3fn_values(x_bytes) * x_scale.astype(np.float64), h_attn, Wu, bu, g_norm, Wf, b_out)

from contextlib import ExitStack

import concourse.mybir as mybir
from concourse.masks import make_identity

F32 = mybir.dt.float32
BF16 = mybir.dt.bfloat16
U32 = mybir.dt.uint32
U8 = mybir.dt.uint8
FP8 = mybir.dt.float8_e4m3fn
FP8X4 = mybir.dt.float8_e4m3fn_x4
MULT = mybir.AluOpType.mult
ADD = mybir.AluOpType.add
POW = mybir.AluOpType.pow
ACT = mybir.ActivationFunctionType

TOKENS = 8192
D = 512
P = 128
NI = 4
GROUP = P * NI
GROUPS = TOKENS // GROUP
EPS = 1.1920928955078125e-07
FLOPS = 2 * 2 * TOKENS * D * D
BYTES = TOKENS * D * (1 + 2 + 4) + 2 * 2 * D * D + 4 * D + 3 * 2 * D

GAIN_ENGINE = ("g", "g", "g", "g")


def tile_hstu_pb_t_kernel(tc, x_bytes, x_scale, h_attn, Wu, bu, g_norm, Wf, b_out, out):
    nc = tc.nc
    xv = x_bytes.flatten_outer_dims().rearrange("(g p i) c -> g p i c", p=P, i=NI)
    hv = h_attn.flatten_outer_dims().rearrange("(g p i) c -> g p i c", p=P, i=NI)
    ov = out.flatten_outer_dims().rearrange("(g p i) c -> g p i c", p=P, i=NI)

    with ExitStack() as ctx:
        keep = ctx.enter_context(tc.tile_pool(name="keep", bufs=1))
        work = ctx.enter_context(tc.tile_pool(name="work", bufs=2))
        psum = ctx.enter_context(tc.psum_pool(name="psum", bufs=2))
        ctx.enter_context(tc.manual_schedule())

        ident = keep.tile([P, P], F32, name="ident")
        rows = keep.tile([P, P], BF16, name="rows")
        idb = keep.tile([P, P], BF16, name="idb")
        vec = keep.tile([P, 8], F32, name="vec")
        scale4 = keep.tile([P, 2, D], F32, name="scale4")
        bo = keep.tile([P, D], BF16, name="bo")
        mhalf = keep.tile([P, NI], F32, name="mhalf")
        warm = keep.tile([P, 1], F32, name="warm")
        wraw = {k: keep.tile([P, NI, D], BF16, name="raw" + k) for k in ("u", "f")}
        wc = {k: keep.tile([P, D], U32, name="wc" + k, align_bytes=64) for k in ("u", "f")}
        ws = {k: keep.tile([P, D], U8, name="ws" + k, align_bytes=64) for k in ("u", "f")}
        xb = [keep.tile([P, NI, D], U8, name="xb%d" % g) for g in range(GROUPS)]
        hb = [keep.tile([P, NI, D], BF16, name="hb%d" % g) for g in range(GROUPS)]

        nc.vector.memset(warm[:], 0.0)
        nc.vector.memset(rows[:], 0.0)
        nc.gpsimd.memset(mhalf[:], -0.5)
        nc.scalar.dma_start(out=scale4[:, 0, :], in_=x_scale.rearrange("a b k -> (a b k)").partition_broadcast(P))
        nc.sync.dma_start(out=xb[0][:], in_=xv[0])
        nc.sync.dma_start(out=wraw["u"][:], in_=Wu.rearrange("(i p) k -> p i k", p=P))
        nc.sync.dma_start(out=rows[0:4, :], in_=bu.rearrange("(t p) -> t p", p=P))
        nc.sync.dma_start(out=rows[4:8, :], in_=g_norm.rearrange("(t p) -> t p", p=P))
        nc.sync.dma_start(out=hb[0][:], in_=hv[0])
        nc.sync.dma_start(out=xb[1][:], in_=xv[1])
        nc.sync.dma_start(out=hb[1][:], in_=hv[1])
        nc.sync.dma_start(out=xb[2][:], in_=xv[2])
        nc.sync.dma_start(out=wraw["f"][:], in_=Wf.rearrange("(i p) k -> p i k", p=P))
        nc.sync.dma_start(out=hb[2][:], in_=hv[2])
        nc.sync.dma_start(out=bo[:], in_=b_out.partition_broadcast(P))
        for g in range(3, GROUPS):
            nc.sync.dma_start(out=xb[g][:], in_=xv[g])
            nc.sync.dma_start(out=hb[g][:], in_=hv[g])

        nc.scalar.activation(out=warm[:], in_=warm[:], func=ACT.Silu)
        nc.scalar.copy(out=scale4[:, 1, :], in_=scale4[:, 0, :])
        make_identity(nc, ident[:])
        make_identity(nc, idb[:])

        live = {}

        def x_scale_half(g, half):
            if half == 0:
                live["xs", g] = work.tile([P, NI * D], BF16, name="xs", bufs=2)
            w = slice(half * 2 * D, (half + 1) * 2 * D)
            nc.vector.tensor_tensor(out=live["xs", g][:, w], in0=xb[g][:].rearrange("p i k -> p (i k)")[:, w].bitcast(FP8), in1=scale4[:].rearrange("p i k -> p (i k)"), op=MULT)

        def square(g, i):
            if i == 0:
                live["ss", g] = work.tile([P, NI], F32, name="ss", bufs=4)
            junk = work.tile([P, D], BF16, name="junk")
            nc.scalar.activation(out=junk[:], in_=hb[g][:, i, :], func=ACT.Square, accum_out=live["ss", g][:, i : i + 1])
            if i == NI - 1:
                ms = work.tile([P, NI], F32, name="ms")
                rstd = work.tile([P, NI], F32, name="rstd", bufs=4)
                nc.gpsimd.tensor_scalar(out=ms[:], in0=live["ss", g][:], scalar1=1.0 / D, scalar2=EPS, op0=MULT, op1=ADD)
                nc.gpsimd.tensor_tensor(out=rstd[:], in0=ms[:], in1=mhalf[:], op=POW)
                live["rstd", g] = rstd

        def turn(src, half, key, g):
            if half == 0:
                live[key, g] = work.tile([P, NI * D], BF16, name="grouped_" + key, align_bytes=64, bufs=1 if key[0] == "w" else 2)
            bank = psum.tile([P, D], F32, name="turn")
            for i in range(2):
                words = src[:, (2 * half + i) * D : (2 * half + i + 1) * D].bitcast(F32)
                for u in range(2):
                    c = (2 * i + u) * P
                    nc.tensor.transpose(bank[:, c : c + P], words[:, u : 2 * P : 2], ident[:])
            dst = live[key, g][:].bitcast(F32)[:, half * D : (half + 1) * D]
            return dst.rearrange("p (i r u) -> p i r u", i=2, u=2), bank[:].rearrange("p (i u r) -> p i r u", i=2, u=2)

        def quant(key, g, codes, scales):
            nc.vector.quantize_mx(out=codes[:].bitcast(FP8X4), scales=scales[:], in_=live[key, g][:])

        def quant_work(key, g):
            c = work.tile([P, D], U32, name="c_" + key, align_bytes=64)
            s = work.tile([P, D], U8, name="s_" + key, align_bytes=64)
            quant(key, g, c, s)
            live["c_" + key, g] = (c, s)

        def mx(bank, lc, ls, lcols, rc, rs):
            nc.tensor.matmul_mx(out=bank[:], lhsT=lc[:, lcols].bitcast(FP8X4), lhsT_scale=ls[:, lcols],
                                rhs=rc[:].bitcast(FP8X4), rhs_scale=rs[:], start=True, stop=True)

        def first(g, t):
            if t == 0:
                live["u", g] = work.tile([P, NI, D], F32, name="u", bufs=2)
                live["gu", g] = work.tile([P, NI, D], F32, name="gu", bufs=2)
            bank = psum.tile([P, D], F32, name="y")
            c, s = live["c_x", g]
            mx(bank, wc["u"], ws["u"], slice(t * P, (t + 1) * P), c, s)
            return bank

        def silu(g, t, bank):
            nc.scalar.activation(out=live["u", g][:, t, :], in_=bank[:], func=ACT.Silu, bias=vec[:, t : t + 1])

        def gain(g, t):
            dst, src, s = live["gu", g][:, t, :], live["u", g][:, t, :], vec[:, 4 + t : 5 + t]
            e = GAIN_ENGINE[t]
            if e == "v":
                nc.vector.tensor_scalar(out=dst, in0=src, scalar1=s, scalar2=None, op0=MULT)
            elif e == "s":
                nc.scalar.activation(out=dst, in_=src, func=ACT.Copy, scale=s)
            else:
                nc.gpsimd.tensor_scalar(out=dst, in0=src, scalar1=s, scalar2=0.0, op0=MULT, op1=ADD)

        def back(g, i):
            bank = psum.tile([P, D], F32, name="ut")
            for t in range(NI):
                nc.tensor.transpose(bank[:, t * P : (t + 1) * P], live["gu", g][:, t, i * P : (i + 1) * P], ident[:])
            return bank

        def gate(g, i, bank):
            if i == 0:
                live["prod", g] = work.tile([P, NI * D], BF16, name="uv", bufs=3)
            nc.vector.scalar_tensor_tensor(out=live["prod", g][:, i * D : (i + 1) * D], in0=bank[:], scalar=live["rstd", g][:, i : i + 1],
                                           in1=hb[g][:, i, :], op0=MULT, op1=MULT)

        def second(g, i):
            bank = psum.tile([P, D], F32, name="o")
            c, s = live["c_uv", g]
            mx(bank, c, s, slice(i * P, (i + 1) * P), wc["f"], ws["f"])
            return bank

        def finish(g, i, bank):
            if i == 0:
                live["res", g] = work.tile([P, NI, D], F32, name="res", bufs=3)
            res = live["res", g]
            nc.vector.tensor_tensor(out=res[:, i, :], in0=bank[:], in1=bo[:], op=ADD)
            if g == GROUPS - 1:
                nc.sync.dma_start(out=ov[g][:, i, :], in_=res[:, i, :])
            elif i == NI - 1:
                nc.sync.dma_start(out=ov[g], in_=res[:])

        def weight(k):
            for half in range(2):
                dst, src = turn(wraw[k][:].rearrange("p i k -> p (i k)"), half, "w" + k, 0)
                if half == 0:
                    nc.scalar.copy(out=dst, in_=src)
                else:
                    nc.vector.tensor_copy(out=dst, in_=src)
            quant("w" + k, 0, wc[k], ws[k])

        def at(slot, lag):
            g, i = divmod(slot - lag, NI)
            return (g, i) if 0 <= g < GROUPS else None

        for k in range(-7, NI * GROUPS + 12):
            if k == -5:
                weight("u")
                vbank = psum.tile([P, P], BF16, name="turn")
                nc.tensor.transpose(vbank[:], rows[:], idb[:])
                nc.vector.tensor_copy(out=vec[:], in_=vbank[:, 0:8])
            if k == 4:
                weight("f")
            e = at(k, 1)
            if e and GAIN_ENGINE[e[1]] != "g":
                gain(*e)
            y, o, b = at(k, 0), at(k, 12), at(k, 5)
            yb = first(*y) if y else None
            ob = second(*o) if o else None
            ub = back(*b) if b else None
            tb = None
            e = at(k, -5)
            if e and e[1] % 2 == 0:
                tb = turn(live["xs", e[0]], e[1] // 2, "x", e[0])
            e = at(k, 8)
            if e and e[1] % 2 == 0:
                tb = turn(live["prod", e[0]], e[1] // 2, "uv", e[0])
            if y:
                silu(*y, yb)
                if GAIN_ENGINE[y[1]] == "g":
                    gain(*y)
            if tb is not None:
                nc.scalar.copy(out=tb[0], in_=tb[1])
            e = at(k, -7)
            if e and e[1] % 2 == 0:
                x_scale_half(e[0], e[1] // 2)
            e = at(k, -1)
            if e and e[1] == 0:
                quant_work("x", e[0])
            e = at(k, 11)
            if e and e[1] == 0:
                quant_work("uv", e[0])
            if o:
                finish(*o, ob)
            if b:
                gate(*b, ub)
            e = at(k, -2)
            if e:
                square(*e)
